import numpy as np
import ml_dtypes


def mxq(x, axis, fmt="e4m3"):
    dtype, down = {"e4m3": (ml_dtypes.float8_e4m3fn, 7), "e5m2": (ml_dtypes.float8_e5m2, 14)}[fmt]
    v = np.moveaxis(np.asarray(x, np.float32).astype(ml_dtypes.bfloat16).astype(np.float64), axis, -1)
    blocks = v.reshape(v.shape[:-1] + (-1, 32))
    amax = np.abs(blocks).max(-1, keepdims=True)
    byte = np.maximum(np.where(amax > 0, np.frexp(amax)[1] - 1 + 127, 0) - down, 1)
    scale = np.exp2(byte - 127.0)
    codes = (blocks / scale).astype(np.float32).astype(dtype).astype(np.float64)
    return np.moveaxis((codes * scale).reshape(v.shape), -1, axis)


WIDE = False


def mx_kscale(k):
    if not WIDE:
        return np.ones(k)
    levels = np.array([10, -10, 5, -5, 0])
    a = np.random.permutation(np.resize(levels, k // 512 * 4)).reshape(k // 512, 4)
    idx = np.arange(k)
    return np.exp2(a[idx // 512, idx % 128 // 32])


BF16 = ml_dtypes.bfloat16


def bf(x):
    return np.asarray(x, np.float32).astype(BF16)


def f64(x):
    return np.asarray(x).astype(np.float64)


E2M1 = np.array([0.0, 0.5, 1.0, 1.5, 2.0, 3.0, 4.0, 6.0, -0.0, -0.5, -1.0, -1.5, -2.0, -3.0, -4.0, -6.0])


def pack_weight(w, fmt):
    k, n = w.shape
    w = f64(bf(w)).reshape(k // 32, 32, n)
    amax = np.abs(w).max(1)
    if fmt == "e4m3":
        byte = np.frexp(amax)[1] - 1 + 127 - 7
    else:
        mant, ex = np.frexp(amax / 6.0)
        byte = np.where(mant > 0.5, ex, ex - 1) + 127
    byte = np.clip(np.where(amax > 0, byte, 1), 1, 254)
    scaled = (w * np.exp2(127.0 - byte)[:, None, :]).reshape(k, n).astype(np.float32)
    by_word = np.ascontiguousarray(scaled.reshape(k // 512, 128, 4, n).transpose(0, 1, 3, 2))
    if fmt == "e4m3":
        words = by_word.astype(ml_dtypes.float8_e4m3fn).view(np.uint8)
    else:
        c = by_word.astype(ml_dtypes.float4_e2m1fn).view(np.uint8) & 0xF
        words = c[..., 0::2] | (c[..., 1::2] << 4)
    return np.ascontiguousarray(words), np.ascontiguousarray(byte.astype(np.uint8).reshape(k // 512, 16, n))


def unpack_weight(words, scales, fmt):
    g, p, n, _ = words.shape
    if fmt == "e4m3":
        vals = np.ascontiguousarray(words).view(ml_dtypes.float8_e4m3fn).astype(np.float64)
    else:
        nib = np.empty((g, p, n, 4), np.uint8)
        nib[..., 0::2] = words & 0xF
        nib[..., 1::2] = words >> 4
        vals = E2M1[nib]
    vals = vals * np.repeat(np.exp2(scales.astype(np.float64) - 127.0), 8, axis=1)[..., None]
    return vals.transpose(0, 1, 3, 2).reshape(g * 512, n)

def pack4(w):
    words, scales = pack_weight(w, "e2m1")
    return words.reshape(words.shape[0], 128, -1), scales


def unpack4(words, scales):
    return unpack_weight(words.reshape(words.shape[0], 128, -1, 2), scales, "e2m1")


IN_C, OUT_C, N, ND = 512, 512, 4096, 2


def sigmoid(v):
    return 1.0 / (1.0 + np.exp(-v))


def setup_inputs():
    s, t = mx_kscale(IN_C), mx_kscale(OUT_C)
    rn = np.random.standard_normal
    x = bf(rn((IN_C, N)) * s[:, None])
    h_prev_dim0 = bf(rn((OUT_C, N)) * t[:, None])
    h_prev_dim1 = bf(rn((OUT_C, N)) * t[:, None])
    ct0 = bf(rn((OUT_C, N)) * 0.65)
    ct1 = bf(rn((OUT_C, N)) * 0.65)
    w_io = rn((OUT_C, IN_C)) * 0.7 / np.sqrt(IN_C) / s[None, :]
    w_ho = rn((OUT_C, OUT_C)) * 0.7 / np.sqrt(OUT_C) / t[None, :]
    b_o = bf(rn((OUT_C, 1)) * 0.5)
    weighted_sum = bf(0.4 + 0.5 * np.random.random(ND))
    w_io_words, w_io_scales = pack4(np.ascontiguousarray(w_io.T))
    w_ho_words, w_ho_scales = pack4(np.ascontiguousarray(w_ho.T))
    return {"x": x,
            "h_prev_dim0": h_prev_dim0,
            "h_prev_dim1": h_prev_dim1,
            "ct0": ct0,
            "ct1": ct1,
            "w_io_words": w_io_words,
            "w_io_scales": w_io_scales,
            "w_ho_words": w_ho_words,
            "w_ho_scales": w_ho_scales,
            "b_o": b_o,
            "weighted_sum": weighted_sum}


def reference(x, h_prev_dim0, h_prev_dim1, ct0, ct1, w_io_words, w_io_scales, w_ho_words, w_ho_scales, b_o, weighted_sum):
    xo = unpack4(w_io_words, w_io_scales).T @ mxq(f64(x), 0, "e4m3")
    who = unpack4(w_ho_words, w_ho_scales).T
    ws = f64(weighted_sum)

    def hidden(h_prev, c):
        o = sigmoid(xo + (who @ mxq(f64(h_prev), 0, "e4m3")) + f64(b_o))
        return o * np.tanh(f64(c))

    ht0 = hidden(h_prev_dim0, ct0)
    ht1 = hidden(h_prev_dim1, ct1)
    return ht0 * ws[0] + ht1 * ws[1]

@@ -1,0 +1,251 @@
+from contextlib import ExitStack
+
+import concourse.mybir as mybir
+from concourse.masks import make_identity
+
+F32 = mybir.dt.float32
+BF16 = mybir.dt.bfloat16
+I32 = mybir.dt.int32
+U32 = mybir.dt.uint32
+U8 = mybir.dt.uint8
+FP8X4 = mybir.dt.float8_e4m3fn_x4
+FP4X4 = mybir.dt.float4_e2m1fn_x4
+ACT = mybir.ActivationFunctionType
+ALU = mybir.AluOpType
+
+P = 128
+PACK = 4
+CHANNELS = 512
+POSITIONS = 4096
+M_TILES = CHANNELS // P
+BLOCK = 512
+N_BLOCKS = POSITIONS // BLOCK
+LOAD_BLOCKS = 2
+N_LOADS = N_BLOCKS // LOAD_BLOCKS
+LOAD_COLS = LOAD_BLOCKS * BLOCK
+HALF_TILES = M_TILES // 2
+RUN = 4
+ACTIVATIONS = ("x", "h0", "h1")
+DIRECTIONS = (0, 1)
+
+FLOPS = 3 * 2 * CHANNELS * CHANNELS * POSITIONS
+
+
+def tile_mdlstmcellweights_pb_t_kernel(
+    tc,
+    x,
+    h_prev_dim0,
+    h_prev_dim1,
+    ct0,
+    ct1,
+    w_io_words,
+    w_io_scales,
+    w_ho_words,
+    w_ho_scales,
+    b_o,
+    weighted_sum,
+    out,
+):
+    nc = tc.nc
+
+    act_dram = {
+        "x": x.rearrange("(p t) n -> p t n", t=PACK),
+        "h0": h_prev_dim0.rearrange("(p t) n -> p t n", t=PACK),
+        "h1": h_prev_dim1.rearrange("(p t) n -> p t n", t=PACK),
+    }
+    cell_dram = (
+        ct0.rearrange("(m p) n -> p m n", p=P),
+        ct1.rearrange("(m p) n -> p m n", p=P),
+    )
+    out_dram = out.rearrange("(m p) n -> p m n", p=P)
+
+    with ExitStack() as stack:
+        consts = stack.enter_context(tc.tile_pool(name="consts", bufs=1))
+        loads = stack.enter_context(tc.tile_pool(name="loads", bufs=2))
+        groups = stack.enter_context(tc.tile_pool(name="groups", bufs=2))
+        packed = stack.enter_context(tc.tile_pool(name="packed", bufs=2))
+        gates = stack.enter_context(tc.tile_pool(name="gates", bufs=3))
+        psum = stack.enter_context(tc.psum_pool(name="psum", bufs=8))
+        stack.enter_context(tc.manual_schedule())
+
+        act_raw = {}
+        cell_raw = {}
+        grouped = {}
+        codes = {}
+        scales = {}
+        tanh_c = {}
+        gate = {}
+
+        def load_activation(name, load):
+            tile = loads.tile([P, PACK, LOAD_COLS], BF16, name="raw_" + name, tag="raw_" + name)
+            cols = slice(load * LOAD_COLS, (load + 1) * LOAD_COLS)
+            nc.sync.dma_start(out=tile[:], in_=act_dram[name][:, :, cols])
+            act_raw[(name, load)] = tile
+
+        def load_cell(d, load):
+            tile = loads.tile([P, M_TILES, LOAD_COLS], BF16, name="cell_%d" % d, tag="cell_%d" % d)
+            cols = slice(load * LOAD_COLS, (load + 1) * LOAD_COLS)
+            nc.sync.dma_start(out=tile[:], in_=cell_dram[d][:, :, cols])
+            cell_raw[(d, load)] = tile
+
+        def block_cols(block):
+            start = (block % LOAD_BLOCKS) * BLOCK
+            return slice(start, start + BLOCK)
+
+        def regroup(block):
+            load = block // LOAD_BLOCKS
+            for name in ACTIVATIONS:
+                tile = groups.tile(
+                    [P, BLOCK, PACK], BF16, name="grouped_" + name, tag="grouped_" + name, align_bytes=64
+                )
+                src = act_raw[(name, load)][:, :, block_cols(block)]
+                src = src.rearrange("p t (c i) -> p c t i", i=RUN)
+                dst = tile[:].rearrange("p (c i) t -> p c t i", i=RUN)
+                if name == "x":
+                    nc.scalar.copy(out=dst, in_=src)
+                else:
+                    nc.vector.tensor_copy(out=dst, in_=src)
+                grouped[(name, block)] = tile
+            if block % LOAD_BLOCKS == LOAD_BLOCKS - 1 and load + 2 < N_LOADS:
+                for name in ACTIVATIONS:
+                    load_activation(name, load + 2)
+
+        def quantise(block):
+            for name in ACTIVATIONS:
+                words = packed.tile([P, BLOCK], U32, name="codes_" + name, tag="codes_" + name, align_bytes=64)
+                plane = packed.tile([P, BLOCK], U8, name="scales_" + name, tag="scales_" + name, align_bytes=64)
+                nc.vector.quantize_mx(
+                    out=words[:].bitcast(FP8X4),
+                    scales=plane[:],
+                    in_=grouped[(name, block)][:].rearrange("p n t -> p (n t)"),
+                )
+                codes[(name, block)] = words
+                scales[(name, block)] = plane
+
+        def gate_half(block, half):
+            load = block // LOAD_BLOCKS
+            tiles = slice(half * HALF_TILES, (half + 1) * HALF_TILES)
+            for d in DIRECTIONS:
+                tile = gates.tile([P, HALF_TILES, BLOCK], F32, name="tanh_%d" % d, tag="tanh_%d" % d)
+                nc.scalar.activation(
+                    out=tile[:], in_=cell_raw[(d, load)][:, tiles, block_cols(block)], func=ACT.Tanh
+                )
+                tanh_c[(d, block, half)] = tile
+            if half == 1 and block % LOAD_BLOCKS == LOAD_BLOCKS - 1 and load + 2 < N_LOADS:
+                for d in DIRECTIONS:
+                    load_cell(d, load + 2)
+            for d in DIRECTIONS:
+                tile = gates.tile([P, HALF_TILES, BLOCK], F32, name="gate_%d" % d, tag="gate_%d" % d)
+                gate[(d, block, half)] = tile
+            for i in range(HALF_TILES):
+                m = half * HALF_TILES + i
+                word_cols = slice(m * P * 2, (m + 1) * P * 2)
+                plane_cols = slice(m * P, (m + 1) * P)
+                for d in DIRECTIONS:
+                    h = "h%d" % d
+                    acc = psum.tile([P, BLOCK], F32, name="acc", tag="acc")
+                    nc.tensor.matmul_mx(
+                        out=acc[:],
+                        lhsT=w_words["io"][:, word_cols].bitcast(FP4X4),
+                        lhsT_scale=w_planes["io"][:, plane_cols],
+                        rhs=codes[("x", block)][:].bitcast(FP8X4),
+                        rhs_scale=scales[("x", block)][:],
+                        start=True,
+                        stop=False,
+                    )
+                    nc.tensor.matmul_mx(
+                        out=acc[:],
+                        lhsT=w_words["ho"][:, word_cols].bitcast(FP4X4),
+                        lhsT_scale=w_planes["ho"][:, plane_cols],
+                        rhs=codes[(h, block)][:].bitcast(FP8X4),
+                        rhs_scale=scales[(h, block)][:],
+                        start=False,
+                        stop=True,
+                    )
+                    nc.scalar.activation(
+                        out=gate[(d, block, half)][:, i, :],
+                        in_=acc[:],
+                        func=ACT.Sigmoid,
+                        bias=bias[:, m : m + 1],
+                        scale=1.0,
+                    )
+
+        def finish_half(block, half):
+            for d in DIRECTIONS:
+                nc.vector.scalar_tensor_tensor(
+                    out=gate[(d, block, half)][:],
+                    in0=gate[(d, block, half)][:],
+                    scalar=mix[:, d : d + 1],
+                    in1=tanh_c[(d, block, half)][:],
+                    op0=ALU.mult,
+                    op1=ALU.mult,
+                )
+            nc.vector.tensor_tensor(
+                out=gate[(0, block, half)][:],
+                in0=gate[(0, block, half)][:],
+                in1=gate[(1, block, half)][:],
+                op=ALU.add,
+            )
+            tiles = slice(half * HALF_TILES, (half + 1) * HALF_TILES)
+            cols = slice(block * BLOCK, (block + 1) * BLOCK)
+            nc.sync.dma_start(out=out_dram[:, tiles, cols], in_=gate[(0, block, half)][:])
+
+        warm = consts.tile([P, 1], F32, name="warm")
+        nc.vector.memset(warm[:], 0.0)
+        nc.scalar.activation(out=warm[:], in_=warm[:], func=ACT.Sigmoid)
+
+        w_words = {}
+        w_planes = {}
+        for key in ("io", "ho"):
+            w_words[key] = consts.tile([P, 2 * CHANNELS], U8, name="words_" + key, align_bytes=64)
+            w_planes[key] = consts.tile([P, CHANNELS], U8, name="planes_" + key, align_bytes=64)
+            nc.vector.memset(w_planes[key][:].bitcast(I32), 0)
+        bias_rows = consts.tile([P, P], BF16, name="bias_rows")
+        nc.vector.memset(bias_rows[:], 0.0)
+        identity = consts.tile([P, P], BF16, name="identity")
+        make_identity(nc, identity[:])
+
+        load_activation("x", 0)
+        load_activation("h0", 0)
+        for key, words, rows in (("io", w_io_words, w_io_scales), ("ho", w_ho_words, w_ho_scales)):
+            nc.sync.dma_start(
+                out=w_words[key][:].bitcast(I32), in_=words.rearrange("g p b -> (g p) b").bitcast(I32)
+            )
+            rows = rows.rearrange("g q n -> (g q) n")
+            for quadrant in range(4):
+                nc.sync.dma_start(
+                    out=w_planes[key][32 * quadrant : 32 * quadrant + 4, :].bitcast(I32),
+                    in_=rows[4 * quadrant : 4 * quadrant + 4, :].bitcast(I32),
+                )
+        nc.sync.dma_start(out=bias_rows[0:M_TILES, :], in_=b_o.rearrange("(m p) o -> m (p o)", p=P))
+        mix_bf16 = consts.tile([P, 2], BF16, name="mix_bf16")
+        nc.sync.dma_start(out=mix_bf16[:], in_=weighted_sum.partition_broadcast(P))
+        load_cell(0, 0)
+        load_activation("h1", 0)
+        load_cell(1, 0)
+        for name in ACTIVATIONS:
+            load_activation(name, 1)
+        for d in DIRECTIONS:
+            load_cell(d, 1)
+
+        regroup(0)
+        quantise(0)
+
+        bias_t = psum.tile([P, P], BF16, name="bias_t", tag="acc")
+        nc.tensor.transpose(bias_t[:], bias_rows[:], identity[:])
+        bias = consts.tile([P, M_TILES], F32, name="bias")
+        nc.vector.tensor_copy(out=bias[:], in_=bias_t[:, 0:M_TILES])
+        mix = consts.tile([P, 2], F32, name="mix")
+        nc.vector.tensor_copy(out=mix[:], in_=mix_bf16[:])
+
+        for block in range(N_BLOCKS):
+            if block + 1 < N_BLOCKS:
+                regroup(block + 1)
+            gate_half(block, 0)
+            if block > 0:
+                finish_half(block - 1, 1)
+            if block + 1 < N_BLOCKS:
+                quantise(block + 1)
+            gate_half(block, 1)
+            finish_half(block, 0)
+        finish_half(N_BLOCKS - 1, 1)

@@ -20,11 +20,11 @@ POSITIONS = 4096
 M_TILES = CHANNELS // P
 BLOCK = 512
 N_BLOCKS = POSITIONS // BLOCK
-LOAD_BLOCKS = 2
-N_LOADS = N_BLOCKS // LOAD_BLOCKS
-LOAD_COLS = LOAD_BLOCKS * BLOCK
 HALF_TILES = M_TILES // 2
 RUN = 4
+X_VECTOR_COLS = 128
+LOAD_BUFS = 2
+PREP_LEAD = 2
 ACTIVATIONS = ("x", "h0", "h1")
 DIRECTIONS = (0, 1)
 
@@ -61,10 +61,11 @@ def tile_mdlstmcellweights_pb_t_kernel(
 
     with ExitStack() as stack:
         consts = stack.enter_context(tc.tile_pool(name="consts", bufs=1))
-        loads = stack.enter_context(tc.tile_pool(name="loads", bufs=2))
+        loads = stack.enter_context(tc.tile_pool(name="loads", bufs=LOAD_BUFS))
         groups = stack.enter_context(tc.tile_pool(name="groups", bufs=2))
-        packed = stack.enter_context(tc.tile_pool(name="packed", bufs=2))
-        gates = stack.enter_context(tc.tile_pool(name="gates", bufs=3))
+        packed = stack.enter_context(tc.tile_pool(name="packed", bufs=PREP_LEAD + 2))
+        tanhs = stack.enter_context(tc.tile_pool(name="tanhs", bufs=3))
+        gates = stack.enter_context(tc.tile_pool(name="gates", bufs=4))
         psum = stack.enter_context(tc.psum_pool(name="psum", bufs=8))
         stack.enter_context(tc.manual_schedule())
 
@@ -76,39 +77,50 @@ def tile_mdlstmcellweights_pb_t_kernel(
         tanh_c = {}
         gate = {}
 
-        def load_activation(name, load):
-            tile = loads.tile([P, PACK, LOAD_COLS], BF16, name="raw_" + name, tag="raw_" + name)
-            cols = slice(load * LOAD_COLS, (load + 1) * LOAD_COLS)
-            nc.sync.dma_start(out=tile[:], in_=act_dram[name][:, :, cols])
-            act_raw[(name, load)] = tile
-
-        def load_cell(d, load):
-            tile = loads.tile([P, M_TILES, LOAD_COLS], BF16, name="cell_%d" % d, tag="cell_%d" % d)
-            cols = slice(load * LOAD_COLS, (load + 1) * LOAD_COLS)
-            nc.sync.dma_start(out=tile[:], in_=cell_dram[d][:, :, cols])
-            cell_raw[(d, load)] = tile
-
         def block_cols(block):
-            start = (block % LOAD_BLOCKS) * BLOCK
-            return slice(start, start + BLOCK)
+            return slice(block * BLOCK, (block + 1) * BLOCK)
 
-        def regroup(block):
-            load = block // LOAD_BLOCKS
-            for name in ACTIVATIONS:
-                tile = groups.tile(
+        def load_activation(name, block):
+            raw = loads.tile([P, PACK, BLOCK], BF16, name="raw_" + name, tag="raw_" + name)
+            nc.sync.dma_start(out=raw[:], in_=act_dram[name][:, :, block_cols(block)])
+            act_raw[(name, block)] = raw
+
+        def load_cell(d, block):
+            raw = loads.tile([P, M_TILES, BLOCK], BF16, name="cell_%d" % d, tag="cell_%d" % d)
+            nc.sync.dma_start(out=raw[:], in_=cell_dram[d][:, :, block_cols(block)])
+            cell_raw[(d, block)] = raw
+
+        def load_block(block):
+            load_activation("x", block)
+            load_activation("h0", block)
+            load_cell(0, block)
+            load_activation("h1", block)
+            load_cell(1, block)
+
+        def regrouping_views(name, block, cols):
+            src = act_raw[(name, block)][:, :, cols].rearrange("p t (c i) -> p c t i", i=RUN)
+            dst = grouped[(name, block)][:, cols, :].rearrange("p (c i) t -> p c t i", i=RUN)
+            return dst, src
+
+        def regroup_on_scalar(block):
+            grouped[("x", block)] = groups.tile(
+                [P, BLOCK, PACK], BF16, name="grouped_x", tag="grouped_x", align_bytes=64
+            )
+            dst, src = regrouping_views("x", block, slice(0, BLOCK - X_VECTOR_COLS))
+            nc.scalar.copy(out=dst, in_=src)
+
+        def regroup_on_vector(block):
+            dst, src = regrouping_views("x", block, slice(BLOCK - X_VECTOR_COLS, BLOCK))
+            nc.vector.tensor_copy(out=dst, in_=src)
+            for name in ("h0", "h1"):
+                grouped[(name, block)] = groups.tile(
                     [P, BLOCK, PACK], BF16, name="grouped_" + name, tag="grouped_" + name, align_bytes=64
                 )
-                src = act_raw[(name, load)][:, :, block_cols(block)]
-                src = src.rearrange("p t (c i) -> p c t i", i=RUN)
-                dst = tile[:].rearrange("p (c i) t -> p c t i", i=RUN)
-                if name == "x":
-                    nc.scalar.copy(out=dst, in_=src)
-                else:
-                    nc.vector.tensor_copy(out=dst, in_=src)
-                grouped[(name, block)] = tile
-            if block % LOAD_BLOCKS == LOAD_BLOCKS - 1 and load + 2 < N_LOADS:
+                dst, src = regrouping_views(name, block, slice(0, BLOCK))
+                nc.vector.tensor_copy(out=dst, in_=src)
+            if block + LOAD_BUFS < N_BLOCKS:
                 for name in ACTIVATIONS:
-                    load_activation(name, load + 2)
+                    load_activation(name, block + LOAD_BUFS)
 
         def quantise(block):
             for name in ACTIVATIONS:
@@ -122,21 +134,18 @@ def tile_mdlstmcellweights_pb_t_kernel(
                 codes[(name, block)] = words
                 scales[(name, block)] = plane
 
+        def tanh_cell(block, d):
+            result = tanhs.tile([P, M_TILES, BLOCK], F32, name="tanh_%d" % d, tag="tanh_%d" % d)
+            nc.scalar.activation(out=result[:], in_=cell_raw[(d, block)][:], func=ACT.Tanh)
+            tanh_c[(d, block)] = result
+            if block + LOAD_BUFS < N_BLOCKS:
+                load_cell(d, block + LOAD_BUFS)
+
         def gate_half(block, half):
-            load = block // LOAD_BLOCKS
-            tiles = slice(half * HALF_TILES, (half + 1) * HALF_TILES)
             for d in DIRECTIONS:
-                tile = gates.tile([P, HALF_TILES, BLOCK], F32, name="tanh_%d" % d, tag="tanh_%d" % d)
-                nc.scalar.activation(
-                    out=tile[:], in_=cell_raw[(d, load)][:, tiles, block_cols(block)], func=ACT.Tanh
+                gate[(d, block, half)] = gates.tile(
+                    [P, HALF_TILES, BLOCK], F32, name="gate_%d" % d, tag="gate_%d" % d
                 )
-                tanh_c[(d, block, half)] = tile
-            if half == 1 and block % LOAD_BLOCKS == LOAD_BLOCKS - 1 and load + 2 < N_LOADS:
-                for d in DIRECTIONS:
-                    load_cell(d, load + 2)
-            for d in DIRECTIONS:
-                tile = gates.tile([P, HALF_TILES, BLOCK], F32, name="gate_%d" % d, tag="gate_%d" % d)
-                gate[(d, block, half)] = tile
             for i in range(HALF_TILES):
                 m = half * HALF_TILES + i
                 word_cols = slice(m * P * 2, (m + 1) * P * 2)
@@ -170,25 +179,27 @@ def tile_mdlstmcellweights_pb_t_kernel(
                         scale=1.0,
                     )
 
-        def finish_half(block, half):
+        def products(block, half):
+            tiles = slice(half * HALF_TILES, (half + 1) * HALF_TILES)
             for d in DIRECTIONS:
                 nc.vector.scalar_tensor_tensor(
                     out=gate[(d, block, half)][:],
                     in0=gate[(d, block, half)][:],
                     scalar=mix[:, d : d + 1],
-                    in1=tanh_c[(d, block, half)][:],
+                    in1=tanh_c[(d, block)][:, tiles, :],
                     op0=ALU.mult,
                     op1=ALU.mult,
                 )
+
+        def total(block, half):
+            tiles = slice(half * HALF_TILES, (half + 1) * HALF_TILES)
             nc.vector.tensor_tensor(
                 out=gate[(0, block, half)][:],
                 in0=gate[(0, block, half)][:],
                 in1=gate[(1, block, half)][:],
                 op=ALU.add,
             )
-            tiles = slice(half * HALF_TILES, (half + 1) * HALF_TILES)
-            cols = slice(block * BLOCK, (block + 1) * BLOCK)
-            nc.sync.dma_start(out=out_dram[:, tiles, cols], in_=gate[(0, block, half)][:])
+            nc.sync.dma_start(out=out_dram[:, tiles, block_cols(block)], in_=gate[(0, block, half)][:])
 
         warm = consts.tile([P, 1], F32, name="warm")
         nc.vector.memset(warm[:], 0.0)
@@ -202,11 +213,14 @@ def tile_mdlstmcellweights_pb_t_kernel(
             nc.vector.memset(w_planes[key][:].bitcast(I32), 0)
         bias_rows = consts.tile([P, P], BF16, name="bias_rows")
         nc.vector.memset(bias_rows[:], 0.0)
+
+        nc.gpsimd.dma_start(out=bias_rows[0:M_TILES, :], in_=b_o.rearrange("(m p) o -> m (p o)", p=P))
+        mix_bf16 = consts.tile([P, 2], BF16, name="mix_bf16")
+        nc.gpsimd.dma_start(out=mix_bf16[:], in_=weighted_sum.partition_broadcast(P))
         identity = consts.tile([P, P], BF16, name="identity")
         make_identity(nc, identity[:])
 
-        load_activation("x", 0)
-        load_activation("h0", 0)
+        load_block(0)
         for key, words, rows in (("io", w_io_words, w_io_scales), ("ho", w_ho_words, w_ho_scales)):
             nc.sync.dma_start(
                 out=w_words[key][:].bitcast(I32), in_=words.rearrange("g p b -> (g p) b").bitcast(I32)
@@ -217,19 +231,13 @@ def tile_mdlstmcellweights_pb_t_kernel(
                     out=w_planes[key][32 * quadrant : 32 * quadrant + 4, :].bitcast(I32),
                     in_=rows[4 * quadrant : 4 * quadrant + 4, :].bitcast(I32),
                 )
-        nc.sync.dma_start(out=bias_rows[0:M_TILES, :], in_=b_o.rearrange("(m p) o -> m (p o)", p=P))
-        mix_bf16 = consts.tile([P, 2], BF16, name="mix_bf16")
-        nc.sync.dma_start(out=mix_bf16[:], in_=weighted_sum.partition_broadcast(P))
-        load_cell(0, 0)
-        load_activation("h1", 0)
-        load_cell(1, 0)
-        for name in ACTIVATIONS:
-            load_activation(name, 1)
-        for d in DIRECTIONS:
-            load_cell(d, 1)
+        load_block(1)
 
-        regroup(0)
+        regroup_on_scalar(0)
+        regroup_on_vector(0)
         quantise(0)
+        for d in DIRECTIONS:
+            tanh_cell(0, d)
 
         bias_t = psum.tile([P, P], BF16, name="bias_t", tag="acc")
         nc.tensor.transpose(bias_t[:], bias_rows[:], identity[:])
@@ -238,14 +246,27 @@ def tile_mdlstmcellweights_pb_t_kernel(
         mix = consts.tile([P, 2], F32, name="mix")
         nc.vector.tensor_copy(out=mix[:], in_=mix_bf16[:])
 
+        for block in range(1, PREP_LEAD):
+            regroup_on_scalar(block)
+            regroup_on_vector(block)
+            quantise(block)
+
         for block in range(N_BLOCKS):
-            if block + 1 < N_BLOCKS:
-                regroup(block + 1)
+            following = block + 1
+            ahead = block + PREP_LEAD
             gate_half(block, 0)
-            if block > 0:
-                finish_half(block - 1, 1)
-            if block + 1 < N_BLOCKS:
-                quantise(block + 1)
+            if following < N_BLOCKS:
+                tanh_cell(following, 0)
+            if ahead < N_BLOCKS:
+                regroup_on_scalar(ahead)
+            products(block, 0)
+            if ahead < N_BLOCKS:
+                regroup_on_vector(ahead)
+            total(block, 0)
             gate_half(block, 1)
-            finish_half(block, 0)
-        finish_half(N_BLOCKS - 1, 1)
+            if following < N_BLOCKS:
+                tanh_cell(following, 1)
+            products(block, 1)
+            if ahead < N_BLOCKS:
+                quantise(ahead)
+            total(block, 1)

@@ -18,6 +18,7 @@ PACK = 4
 CHANNELS = 512
 POSITIONS = 4096
 M_TILES = CHANNELS // P
+assert M_TILES == PACK
 BLOCK = 512
 N_BLOCKS = POSITIONS // BLOCK
 HALF_TILES = M_TILES // 2
@@ -48,16 +49,18 @@ def tile_mdlstmcellweights_pb_t_kernel(
 ):
     nc = tc.nc
 
-    act_dram = {
+    in_dram = {
         "x": x.rearrange("(p t) n -> p t n", t=PACK),
         "h0": h_prev_dim0.rearrange("(p t) n -> p t n", t=PACK),
         "h1": h_prev_dim1.rearrange("(p t) n -> p t n", t=PACK),
+        "c0": ct0.rearrange("(m p) n -> p m n", p=P),
+        "c1": ct1.rearrange("(m p) n -> p m n", p=P),
     }
-    cell_dram = (
-        ct0.rearrange("(m p) n -> p m n", p=P),
-        ct1.rearrange("(m p) n -> p m n", p=P),
-    )
     out_dram = out.rearrange("(m p) n -> p m n", p=P)
+    weight_dram = {
+        "io": (w_io_words.rearrange("g p b -> (g p) b"), w_io_scales.rearrange("g q n -> (g q) n")),
+        "ho": (w_ho_words.rearrange("g p b -> (g p) b"), w_ho_scales.rearrange("g q n -> (g q) n")),
+    }
 
     with ExitStack() as stack:
         consts = stack.enter_context(tc.tile_pool(name="consts", bufs=1))
@@ -69,8 +72,7 @@ def tile_mdlstmcellweights_pb_t_kernel(
         psum = stack.enter_context(tc.psum_pool(name="psum", bufs=8))
         stack.enter_context(tc.manual_schedule())
 
-        act_raw = {}
-        cell_raw = {}
+        raw = {}
         grouped = {}
         codes = {}
         scales = {}
@@ -80,25 +82,24 @@ def tile_mdlstmcellweights_pb_t_kernel(
         def block_cols(block):
             return slice(block * BLOCK, (block + 1) * BLOCK)
 
-        def load_activation(name, block):
-            raw = loads.tile([P, PACK, BLOCK], BF16, name="raw_" + name, tag="raw_" + name)
-            nc.sync.dma_start(out=raw[:], in_=act_dram[name][:, :, block_cols(block)])
-            act_raw[(name, block)] = raw
+        def load_input(name, block):
+            landed = loads.tile([P, PACK, BLOCK], BF16, name="raw_" + name, tag="raw_" + name)
+            nc.sync.dma_start(out=landed[:], in_=in_dram[name][:, :, block_cols(block)])
+            raw[(name, block)] = landed
 
-        def load_cell(d, block):
-            raw = loads.tile([P, M_TILES, BLOCK], BF16, name="cell_%d" % d, tag="cell_%d" % d)
-            nc.sync.dma_start(out=raw[:], in_=cell_dram[d][:, :, block_cols(block)])
-            cell_raw[(d, block)] = raw
-
-        def load_block(block):
-            load_activation("x", block)
-            load_activation("h0", block)
-            load_cell(0, block)
-            load_activation("h1", block)
-            load_cell(1, block)
+        def load_weight_piece(key, piece):
+            words, rows = weight_dram[key]
+            if piece == 0:
+                nc.sync.dma_start(out=w_words[key][:].bitcast(I32), in_=words.bitcast(I32))
+            else:
+                quadrant = piece - 1
+                nc.sync.dma_start(
+                    out=w_planes[key][32 * quadrant : 32 * quadrant + 4, :].bitcast(I32),
+                    in_=rows[4 * quadrant : 4 * quadrant + 4, :].bitcast(I32),
+                )
 
         def regrouping_views(name, block, cols):
-            src = act_raw[(name, block)][:, :, cols].rearrange("p t (c i) -> p c t i", i=RUN)
+            src = raw[(name, block)][:, :, cols].rearrange("p t (c i) -> p c t i", i=RUN)
             dst = grouped[(name, block)][:, cols, :].rearrange("p (c i) t -> p c t i", i=RUN)
             return dst, src
 
@@ -120,7 +121,7 @@ def tile_mdlstmcellweights_pb_t_kernel(
                 nc.vector.tensor_copy(out=dst, in_=src)
             if block + LOAD_BUFS < N_BLOCKS:
                 for name in ACTIVATIONS:
-                    load_activation(name, block + LOAD_BUFS)
+                    load_input(name, block + LOAD_BUFS)
 
         def quantise(block):
             for name in ACTIVATIONS:
@@ -136,22 +137,22 @@ def tile_mdlstmcellweights_pb_t_kernel(
 
         def tanh_cell(block, d):
             result = tanhs.tile([P, M_TILES, BLOCK], F32, name="tanh_%d" % d, tag="tanh_%d" % d)
-            nc.scalar.activation(out=result[:], in_=cell_raw[(d, block)][:], func=ACT.Tanh)
+            nc.scalar.activation(out=result[:], in_=raw[("c%d" % d, block)][:], func=ACT.Tanh)
             tanh_c[(d, block)] = result
             if block + LOAD_BUFS < N_BLOCKS:
-                load_cell(d, block + LOAD_BUFS)
+                load_input("c%d" % d, block + LOAD_BUFS)
 
         def gate_half(block, half):
             for d in DIRECTIONS:
                 gate[(d, block, half)] = gates.tile(
                     [P, HALF_TILES, BLOCK], F32, name="gate_%d" % d, tag="gate_%d" % d
                 )
-            for i in range(HALF_TILES):
-                m = half * HALF_TILES + i
-                word_cols = slice(m * P * 2, (m + 1) * P * 2)
-                plane_cols = slice(m * P, (m + 1) * P)
-                for d in DIRECTIONS:
-                    h = "h%d" % d
+            for d in DIRECTIONS:
+                h = "h%d" % d
+                for i in range(HALF_TILES):
+                    m = half * HALF_TILES + i
+                    word_cols = slice(m * P * 2, (m + 1) * P * 2)
+                    plane_cols = slice(m * P, (m + 1) * P)
                     acc = psum.tile([P, BLOCK], F32, name="acc", tag="acc")
                     nc.tensor.matmul_mx(
                         out=acc[:],
@@ -220,18 +221,12 @@ def tile_mdlstmcellweights_pb_t_kernel(
         identity = consts.tile([P, P], BF16, name="identity")
         make_identity(nc, identity[:])
 
-        load_block(0)
-        for key, words, rows in (("io", w_io_words, w_io_scales), ("ho", w_ho_words, w_ho_scales)):
-            nc.sync.dma_start(
-                out=w_words[key][:].bitcast(I32), in_=words.rearrange("g p b -> (g p) b").bitcast(I32)
-            )
-            rows = rows.rearrange("g q n -> (g q) n")
-            for quadrant in range(4):
-                nc.sync.dma_start(
-                    out=w_planes[key][32 * quadrant : 32 * quadrant + 4, :].bitcast(I32),
-                    in_=rows[4 * quadrant : 4 * quadrant + 4, :].bitcast(I32),
-                )
-        load_block(1)
+        for piece, name in enumerate(("x", "h0", "c0", "h1", "c1")):
+            load_input(name, 0)
+            for key in ("io", "ho"):
+                load_weight_piece(key, piece)
+        for name in ("x", "h0", "h1", "c0", "c1"):
+            load_input(name, 1)
 
         regroup_on_scalar(0)
         regroup_on_vector(0)

@@ -1,7 +1,6 @@
 from contextlib import ExitStack
 
 import concourse.mybir as mybir
-from concourse.masks import make_identity
 
 F32 = mybir.dt.float32
 BF16 = mybir.dt.bfloat16
@@ -23,7 +22,7 @@ BLOCK = 512
 N_BLOCKS = POSITIONS // BLOCK
 HALF_TILES = M_TILES // 2
 RUN = 4
-X_VECTOR_COLS = 128
+X_VECTOR_COLS = 64
 LOAD_BUFS = 2
 PREP_LEAD = 2
 ACTIVATIONS = ("x", "h0", "h1")
@@ -142,65 +141,78 @@ def tile_mdlstmcellweights_pb_t_kernel(
             if block + LOAD_BUFS < N_BLOCKS:
                 load_input("c%d" % d, block + LOAD_BUFS)
 
-        def gate_half(block, half):
-            for d in DIRECTIONS:
+        def gate_tile(block, d, m):
+            half, i = divmod(m, HALF_TILES)
+            if (d, block, half) not in gate:
                 gate[(d, block, half)] = gates.tile(
                     [P, HALF_TILES, BLOCK], F32, name="gate_%d" % d, tag="gate_%d" % d
                 )
+            h = "h%d" % d
+            word_cols = slice(m * P * 2, (m + 1) * P * 2)
+            plane_cols = slice(m * P, (m + 1) * P)
+            acc = psum.tile([P, BLOCK], F32, name="acc", tag="acc")
+            nc.tensor.matmul_mx(
+                out=acc[:],
+                lhsT=w_words["io"][:, word_cols].bitcast(FP4X4),
+                lhsT_scale=w_planes["io"][:, plane_cols],
+                rhs=codes[("x", block)][:].bitcast(FP8X4),
+                rhs_scale=scales[("x", block)][:],
+                start=True,
+                stop=False,
+            )
+            nc.tensor.matmul_mx(
+                out=acc[:],
+                lhsT=w_words["ho"][:, word_cols].bitcast(FP4X4),
+                lhsT_scale=w_planes["ho"][:, plane_cols],
+                rhs=codes[(h, block)][:].bitcast(FP8X4),
+                rhs_scale=scales[(h, block)][:],
+                start=False,
+                stop=True,
+            )
+            nc.scalar.activation(
+                out=gate[(d, block, half)][:, i, :],
+                in_=acc[:],
+                func=ACT.Sigmoid,
+                bias=bias[:, m : m + 1],
+                scale=1.0,
+            )
+
+        def gate_half(block, half):
             for d in DIRECTIONS:
-                h = "h%d" % d
                 for i in range(HALF_TILES):
-                    m = half * HALF_TILES + i
-                    word_cols = slice(m * P * 2, (m + 1) * P * 2)
-                    plane_cols = slice(m * P, (m + 1) * P)
-                    acc = psum.tile([P, BLOCK], F32, name="acc", tag="acc")
-                    nc.tensor.matmul_mx(
-                        out=acc[:],
-                        lhsT=w_words["io"][:, word_cols].bitcast(FP4X4),
-                        lhsT_scale=w_planes["io"][:, plane_cols],
-                        rhs=codes[("x", block)][:].bitcast(FP8X4),
-                        rhs_scale=scales[("x", block)][:],
-                        start=True,
-                        stop=False,
-                    )
-                    nc.tensor.matmul_mx(
-                        out=acc[:],
-                        lhsT=w_words["ho"][:, word_cols].bitcast(FP4X4),
-                        lhsT_scale=w_planes["ho"][:, plane_cols],
-                        rhs=codes[(h, block)][:].bitcast(FP8X4),
-                        rhs_scale=scales[(h, block)][:],
-                        start=False,
-                        stop=True,
-                    )
-                    nc.scalar.activation(
-                        out=gate[(d, block, half)][:, i, :],
-                        in_=acc[:],
-                        func=ACT.Sigmoid,
-                        bias=bias[:, m : m + 1],
-                        scale=1.0,
-                    )
+                    gate_tile(block, d, half * HALF_TILES + i)
+
+        def tanh_tile(block, d, m):
+            if (d, block) not in tanh_c:
+                tanh_c[(d, block)] = tanhs.tile([P, M_TILES, BLOCK], F32, name="tanh_%d" % d, tag="tanh_%d" % d)
+            nc.scalar.activation(
+                out=tanh_c[(d, block)][:, m, :], in_=raw[("c%d" % d, block)][:, m, :], func=ACT.Tanh
+            )
+
+        def product(block, d, half, first=0, last=HALF_TILES):
+            tiles = slice(half * HALF_TILES + first, half * HALF_TILES + last)
+            nc.vector.scalar_tensor_tensor(
+                out=gate[(d, block, half)][:, first:last, :],
+                in0=gate[(d, block, half)][:, first:last, :],
+                scalar=mix[:, d : d + 1],
+                in1=tanh_c[(d, block)][:, tiles, :],
+                op0=ALU.mult,
+                op1=ALU.mult,
+            )
 
         def products(block, half):
-            tiles = slice(half * HALF_TILES, (half + 1) * HALF_TILES)
             for d in DIRECTIONS:
-                nc.vector.scalar_tensor_tensor(
-                    out=gate[(d, block, half)][:],
-                    in0=gate[(d, block, half)][:],
-                    scalar=mix[:, d : d + 1],
-                    in1=tanh_c[(d, block)][:, tiles, :],
-                    op0=ALU.mult,
-                    op1=ALU.mult,
-                )
+                product(block, d, half)
 
-        def total(block, half):
-            tiles = slice(half * HALF_TILES, (half + 1) * HALF_TILES)
+        def total(block, half, first=0, last=HALF_TILES):
+            tiles = slice(half * HALF_TILES + first, half * HALF_TILES + last)
             nc.vector.tensor_tensor(
-                out=gate[(0, block, half)][:],
-                in0=gate[(0, block, half)][:],
-                in1=gate[(1, block, half)][:],
+                out=gate[(0, block, half)][:, first:last, :],
+                in0=gate[(0, block, half)][:, first:last, :],
+                in1=gate[(1, block, half)][:, first:last, :],
                 op=ALU.add,
             )
-            nc.sync.dma_start(out=out_dram[:, tiles, block_cols(block)], in_=gate[(0, block, half)][:])
+            nc.sync.dma_start(out=out_dram[:, tiles, block_cols(block)], in_=gate[(0, block, half)][:, first:last, :])
 
         warm = consts.tile([P, 1], F32, name="warm")
         nc.vector.memset(warm[:], 0.0)
@@ -214,15 +226,20 @@ def tile_mdlstmcellweights_pb_t_kernel(
             nc.vector.memset(w_planes[key][:].bitcast(I32), 0)
         bias_rows = consts.tile([P, P], BF16, name="bias_rows")
         nc.vector.memset(bias_rows[:], 0.0)
-
-        nc.gpsimd.dma_start(out=bias_rows[0:M_TILES, :], in_=b_o.rearrange("(m p) o -> m (p o)", p=P))
-        mix_bf16 = consts.tile([P, 2], BF16, name="mix_bf16")
-        nc.gpsimd.dma_start(out=mix_bf16[:], in_=weighted_sum.partition_broadcast(P))
-        identity = consts.tile([P, P], BF16, name="identity")
-        make_identity(nc, identity[:])
+        mix_row = consts.tile([P, 2], BF16, name="mix_row")
+        nc.vector.memset(mix_row[:], 0.0)
+        ones = consts.tile([P, P], BF16, name="ones")
+        nc.vector.memset(ones[:], 1.0)
+        pick = consts.tile([P, M_TILES], BF16, name="pick")
+        nc.vector.memset(pick[:], 0.0)
+        for m in range(M_TILES):
+            nc.vector.memset(pick[32 * m : 32 * (m + 1), m : m + 1], 1.0)
 
         for piece, name in enumerate(("x", "h0", "c0", "h1", "c1")):
             load_input(name, 0)
+            if piece == 0:
+                nc.sync.dma_start(out=bias_rows[0:P:32, :], in_=b_o.rearrange("(m p) o -> m (p o)", p=P))
+                nc.sync.dma_start(out=mix_row[0:1, :], in_=weighted_sum.rearrange("(o d) -> o d", o=1))
             for key in ("io", "ho"):
                 load_weight_piece(key, piece)
         for name in ("x", "h0", "h1", "c0", "c1"):
@@ -234,23 +251,25 @@ def tile_mdlstmcellweights_pb_t_kernel(
         for d in DIRECTIONS:
             tanh_cell(0, d)
 
-        bias_t = psum.tile([P, P], BF16, name="bias_t", tag="acc")
-        nc.tensor.transpose(bias_t[:], bias_rows[:], identity[:])
-        bias = consts.tile([P, M_TILES], F32, name="bias")
-        nc.vector.tensor_copy(out=bias[:], in_=bias_t[:, 0:M_TILES])
-        mix = consts.tile([P, 2], F32, name="mix")
-        nc.vector.tensor_copy(out=mix[:], in_=mix_bf16[:])
+        spread = psum.tile([P, M_TILES + 2], F32, name="spread", tag="acc")
+        nc.tensor.matmul(out=spread[:, 0:M_TILES], lhsT=bias_rows[:], rhs=pick[:], start=True, stop=True)
+        nc.tensor.matmul(out=spread[:, M_TILES : M_TILES + 2], lhsT=ones[:], rhs=mix_row[:], start=True, stop=True)
+        small = consts.tile([P, M_TILES + 2], F32, name="small")
+        nc.vector.tensor_copy(out=small[:], in_=spread[:])
+        bias = small[:, 0:M_TILES]
+        mix = small[:, M_TILES : M_TILES + 2]
 
         for block in range(1, PREP_LEAD):
             regroup_on_scalar(block)
             regroup_on_vector(block)
             quantise(block)
 
-        for block in range(N_BLOCKS):
+        LAST = N_BLOCKS - 1
+        for block in range(LAST):
             following = block + 1
             ahead = block + PREP_LEAD
             gate_half(block, 0)
-            if following < N_BLOCKS:
+            if following < LAST:
                 tanh_cell(following, 0)
             if ahead < N_BLOCKS:
                 regroup_on_scalar(ahead)
@@ -259,9 +278,21 @@ def tile_mdlstmcellweights_pb_t_kernel(
                 regroup_on_vector(ahead)
             total(block, 0)
             gate_half(block, 1)
-            if following < N_BLOCKS:
+            if following < LAST:
                 tanh_cell(following, 1)
             products(block, 1)
             if ahead < N_BLOCKS:
                 quantise(ahead)
             total(block, 1)
+
+        for m in range(M_TILES):
+            half, i = divmod(m, HALF_TILES)
+            for d in DIRECTIONS:
+                tanh_tile(LAST, d, m)
+            for d in DIRECTIONS:
+                gate_tile(LAST, d, m)
+            product(LAST, 0, half, i, i + 1)
+            if m > 0:
+                total(LAST, (m - 1) // HALF_TILES, (m - 1) % HALF_TILES, (m - 1) % HALF_TILES + 1)
+            product(LAST, 1, half, i, i + 1)
+        total(LAST, 1, HALF_TILES - 1, HALF_TILES)

@@ -22,7 +22,7 @@ BLOCK = 512
 N_BLOCKS = POSITIONS // BLOCK
 HALF_TILES = M_TILES // 2
 RUN = 4
-X_VECTOR_COLS = 64
+X_VECTOR_COLS = 0
 LOAD_BUFS = 2
 PREP_LEAD = 2
 ACTIVATIONS = ("x", "h0", "h1")
@@ -102,16 +102,21 @@ def tile_mdlstmcellweights_pb_t_kernel(
             dst = grouped[(name, block)][:, cols, :].rearrange("p (c i) t -> p c t i", i=RUN)
             return dst, src
 
+        def x_vector_cols(block):
+            return BLOCK if block < PREP_LEAD else X_VECTOR_COLS
+
         def regroup_on_scalar(block):
             grouped[("x", block)] = groups.tile(
                 [P, BLOCK, PACK], BF16, name="grouped_x", tag="grouped_x", align_bytes=64
             )
-            dst, src = regrouping_views("x", block, slice(0, BLOCK - X_VECTOR_COLS))
-            nc.scalar.copy(out=dst, in_=src)
+            if x_vector_cols(block) < BLOCK:
+                dst, src = regrouping_views("x", block, slice(0, BLOCK - x_vector_cols(block)))
+                nc.scalar.copy(out=dst, in_=src)
 
         def regroup_on_vector(block):
-            dst, src = regrouping_views("x", block, slice(BLOCK - X_VECTOR_COLS, BLOCK))
-            nc.vector.tensor_copy(out=dst, in_=src)
+            if x_vector_cols(block) > 0:
+                dst, src = regrouping_views("x", block, slice(BLOCK - x_vector_cols(block), BLOCK))
+                nc.vector.tensor_copy(out=dst, in_=src)
             for name in ("h0", "h1"):
                 grouped[(name, block)] = groups.tile(
                     [P, BLOCK, PACK], BF16, name="grouped_" + name, tag="grouped_" + name, align_bytes=64
@@ -242,11 +247,12 @@ def tile_mdlstmcellweights_pb_t_kernel(
                 nc.sync.dma_start(out=mix_row[0:1, :], in_=weighted_sum.rearrange("(o d) -> o d", o=1))
             for key in ("io", "ho"):
                 load_weight_piece(key, piece)
-        for name in ("x", "h0", "h1", "c0", "c1"):
+        for name in ("x", "h0", "h1", "c0"):
             load_input(name, 1)
 
         regroup_on_scalar(0)
         regroup_on_vector(0)
+        load_input("c1", 1)
         quantise(0)
         for d in DIRECTIONS:
             tanh_cell(0, d)

@@ -1,6 +1,7 @@
 from contextlib import ExitStack
 
 import concourse.mybir as mybir
+from concourse.masks import make_identity
 
 F32 = mybir.dt.float32
 BF16 = mybir.dt.bfloat16
@@ -22,7 +23,9 @@ BLOCK = 512
 N_BLOCKS = POSITIONS // BLOCK
 HALF_TILES = M_TILES // 2
 RUN = 4
-X_VECTOR_COLS = 0
+X_BANK = 256
+GATE_BANKS = 6
+H1_SCALAR_COLS = 128
 LOAD_BUFS = 2
 PREP_LEAD = 2
 ACTIVATIONS = ("x", "h0", "h1")
@@ -68,7 +71,8 @@ def tile_mdlstmcellweights_pb_t_kernel(
         packed = stack.enter_context(tc.tile_pool(name="packed", bufs=PREP_LEAD + 2))
         tanhs = stack.enter_context(tc.tile_pool(name="tanhs", bufs=3))
         gates = stack.enter_context(tc.tile_pool(name="gates", bufs=4))
-        psum = stack.enter_context(tc.psum_pool(name="psum", bufs=8))
+        psum = stack.enter_context(tc.psum_pool(name="psum", bufs=GATE_BANKS))
+        xpsum = stack.enter_context(tc.psum_pool(name="xpsum", bufs=BLOCK // X_BANK))
         stack.enter_context(tc.manual_schedule())
 
         raw = {}
@@ -102,29 +106,49 @@ def tile_mdlstmcellweights_pb_t_kernel(
             dst = grouped[(name, block)][:, cols, :].rearrange("p (c i) t -> p c t i", i=RUN)
             return dst, src
 
-        def x_vector_cols(block):
-            return BLOCK if block < PREP_LEAD else X_VECTOR_COLS
-
-        def regroup_on_scalar(block):
-            grouped[("x", block)] = groups.tile(
-                [P, BLOCK, PACK], BF16, name="grouped_x", tag="grouped_x", align_bytes=64
-            )
-            if x_vector_cols(block) < BLOCK:
-                dst, src = regrouping_views("x", block, slice(0, BLOCK - x_vector_cols(block)))
-                nc.scalar.copy(out=dst, in_=src)
-
-        def regroup_on_vector(block):
-            if x_vector_cols(block) > 0:
-                dst, src = regrouping_views("x", block, slice(BLOCK - x_vector_cols(block), BLOCK))
-                nc.vector.tensor_copy(out=dst, in_=src)
-            for name in ("h0", "h1"):
+        def grouped_tile(name, block):
+            if (name, block) not in grouped:
                 grouped[(name, block)] = groups.tile(
                     [P, BLOCK, PACK], BF16, name="grouped_" + name, tag="grouped_" + name, align_bytes=64
                 )
-                dst, src = regrouping_views(name, block, slice(0, BLOCK))
+            return grouped[(name, block)]
+
+        def h1_scalar_cols(block):
+            return 0 if block < PREP_LEAD else H1_SCALAR_COLS
+
+        def regroup_x(block):
+            flat = grouped_tile("x", block)[:].rearrange("p n t -> p (n t)")
+            banks = {}
+            for j in range(BLOCK // X_BANK):
+                bank = xpsum.tile([P, X_BANK * PACK], BF16, name="xbank", tag="xbank")
+                for i in range(X_BANK // P):
+                    cols = slice(j * X_BANK + i * P, j * X_BANK + (i + 1) * P)
+                    nc.tensor.matmul(
+                        out=bank[:, i * P * PACK : (i + 1) * P * PACK],
+                        lhsT=ident[:],
+                        rhs=raw[("x", block)][:, :, cols].rearrange("p t n -> p n t"),
+                        start=True,
+                        stop=True,
+                    )
+                banks[j] = bank
+            if block + LOAD_BUFS < N_BLOCKS:
+                load_input("x", block + LOAD_BUFS)
+            for j in range(BLOCK // X_BANK):
+                nc.scalar.copy(out=flat[:, j * X_BANK * PACK : (j + 1) * X_BANK * PACK], in_=banks[j][:])
+            if h1_scalar_cols(block) > 0:
+                grouped_tile("h1", block)
+                dst, src = regrouping_views("h1", block, slice(0, h1_scalar_cols(block)))
+                nc.scalar.copy(out=dst, in_=src)
+
+        def regroup_on_vector(block):
+            names = ACTIVATIONS if block < PREP_LEAD else ("h0", "h1")
+            for name in names:
+                grouped_tile(name, block)
+                first = h1_scalar_cols(block) if name == "h1" else 0
+                dst, src = regrouping_views(name, block, slice(first, BLOCK))
                 nc.vector.tensor_copy(out=dst, in_=src)
             if block + LOAD_BUFS < N_BLOCKS:
-                for name in ACTIVATIONS:
+                for name in names:
                     load_input(name, block + LOAD_BUFS)
 
         def quantise(block):
@@ -235,6 +259,8 @@ def tile_mdlstmcellweights_pb_t_kernel(
         nc.vector.memset(mix_row[:], 0.0)
         ones = consts.tile([P, P], BF16, name="ones")
         nc.vector.memset(ones[:], 1.0)
+        ident = consts.tile([P, P], BF16, name="ident")
+        make_identity(nc, ident[:])
         pick = consts.tile([P, M_TILES], BF16, name="pick")
         nc.vector.memset(pick[:], 0.0)
         for m in range(M_TILES):
@@ -250,7 +276,6 @@ def tile_mdlstmcellweights_pb_t_kernel(
         for name in ("x", "h0", "h1", "c0"):
             load_input(name, 1)
 
-        regroup_on_scalar(0)
         regroup_on_vector(0)
         load_input("c1", 1)
         quantise(0)
@@ -266,7 +291,6 @@ def tile_mdlstmcellweights_pb_t_kernel(
         mix = small[:, M_TILES : M_TILES + 2]
 
         for block in range(1, PREP_LEAD):
-            regroup_on_scalar(block)
             regroup_on_vector(block)
             quantise(block)
 
@@ -278,7 +302,7 @@ def tile_mdlstmcellweights_pb_t_kernel(
             if following < LAST:
                 tanh_cell(following, 0)
             if ahead < N_BLOCKS:
-                regroup_on_scalar(ahead)
+                regroup_x(ahead)
             products(block, 0)
             if ahead < N_BLOCKS:
                 regroup_on_vector(ahead)

@@ -26,6 +26,7 @@ RUN = 4
 X_BANK = 256
 GATE_BANKS = 6
 H1_SCALAR_COLS = 128
+FIRST_TENSOR = 3
 LOAD_BUFS = 2
 PREP_LEAD = 2
 ACTIVATIONS = ("x", "h0", "h1")
@@ -114,10 +115,15 @@ def tile_mdlstmcellweights_pb_t_kernel(
             return grouped[(name, block)]
 
         def h1_scalar_cols(block):
-            return 0 if block < PREP_LEAD else H1_SCALAR_COLS
+            return 0 if block < FIRST_TENSOR else H1_SCALAR_COLS
 
         def regroup_x(block):
             flat = grouped_tile("x", block)[:].rearrange("p n t -> p (n t)")
+            if block < FIRST_TENSOR:
+                dst, src = regrouping_views("x", block, slice(0, BLOCK))
+                nc.scalar.copy(out=dst, in_=src)
+                load_input("x", block + LOAD_BUFS)
+                return
             banks = {}
             for j in range(BLOCK // X_BANK):
                 bank = xpsum.tile([P, X_BANK * PACK], BF16, name="xbank", tag="xbank")

@@ -25,7 +25,7 @@ HALF_TILES = M_TILES // 2
 RUN = 4
 X_BANK = 256
 GATE_BANKS = 6
-H1_SCALAR_COLS = 128
+H1_SCALAR_COLS = 160
 FIRST_TENSOR = 3
 LOAD_BUFS = 2
 PREP_LEAD = 2

@@ -24,8 +24,10 @@ N_BLOCKS = POSITIONS // BLOCK
 HALF_TILES = M_TILES // 2
 RUN = 4
 X_BANK = 256
-GATE_BANKS = 6
-H1_SCALAR_COLS = 160
+GATE_BANKS = 5
+H1_SCALAR_COLS = 0
+SHARE_EARLY = 0
+H1_TENSOR_COLS = 256
 FIRST_TENSOR = 3
 LOAD_BUFS = 2
 PREP_LEAD = 2
@@ -73,7 +75,7 @@ def tile_mdlstmcellweights_pb_t_kernel(
         tanhs = stack.enter_context(tc.tile_pool(name="tanhs", bufs=3))
         gates = stack.enter_context(tc.tile_pool(name="gates", bufs=4))
         psum = stack.enter_context(tc.psum_pool(name="psum", bufs=GATE_BANKS))
-        xpsum = stack.enter_context(tc.psum_pool(name="xpsum", bufs=BLOCK // X_BANK))
+        xpsum = stack.enter_context(tc.psum_pool(name="xpsum", bufs=8 - GATE_BANKS))
         stack.enter_context(tc.manual_schedule())
 
         raw = {}
@@ -114,47 +116,72 @@ def tile_mdlstmcellweights_pb_t_kernel(
                 )
             return grouped[(name, block)]
 
+        def h1_tensor_cols(block):
+            return 0 if block < FIRST_TENSOR else H1_TENSOR_COLS
+
         def h1_scalar_cols(block):
             return 0 if block < FIRST_TENSOR else H1_SCALAR_COLS
 
-        def regroup_x(block):
-            flat = grouped_tile("x", block)[:].rearrange("p n t -> p (n t)")
-            if block < FIRST_TENSOR:
-                dst, src = regrouping_views("x", block, slice(0, BLOCK))
-                nc.scalar.copy(out=dst, in_=src)
-                load_input("x", block + LOAD_BUFS)
-                return
+        def regroup_by_tensor(name, block, n_cols):
             banks = {}
-            for j in range(BLOCK // X_BANK):
+            for j in range((n_cols + X_BANK - 1) // X_BANK):
+                width = min(X_BANK, n_cols - j * X_BANK)
                 bank = xpsum.tile([P, X_BANK * PACK], BF16, name="xbank", tag="xbank")
-                for i in range(X_BANK // P):
+                for i in range(width // P):
                     cols = slice(j * X_BANK + i * P, j * X_BANK + (i + 1) * P)
                     nc.tensor.matmul(
                         out=bank[:, i * P * PACK : (i + 1) * P * PACK],
                         lhsT=ident[:],
-                        rhs=raw[("x", block)][:, :, cols].rearrange("p t n -> p n t"),
+                        rhs=raw[(name, block)][:, :, cols].rearrange("p t n -> p n t"),
                         start=True,
                         stop=True,
                     )
-                banks[j] = bank
+                banks[j] = (bank, width)
+            return banks
+
+        def copy_out(name, block, banks):
+            flat = grouped_tile(name, block)[:].rearrange("p n t -> p (n t)")
+            for j in range(len(banks)):
+                bank, width = banks[j]
+                nc.scalar.copy(
+                    out=flat[:, j * X_BANK * PACK : (j * X_BANK + width) * PACK], in_=bank[:, 0 : width * PACK]
+                )
+
+        def regroup_x(block):
+            if block < FIRST_TENSOR:
+                grouped_tile("x", block)
+                dst, src = regrouping_views("x", block, slice(0, BLOCK))
+                nc.scalar.copy(out=dst, in_=src)
+                load_input("x", block + LOAD_BUFS)
+                return
+            banks = regroup_by_tensor("x", block, BLOCK)
             if block + LOAD_BUFS < N_BLOCKS:
                 load_input("x", block + LOAD_BUFS)
-            for j in range(BLOCK // X_BANK):
-                nc.scalar.copy(out=flat[:, j * X_BANK * PACK : (j + 1) * X_BANK * PACK], in_=banks[j][:])
+            copy_out("x", block, banks)
+
+        def scalar_share_of_h1(block):
+            copy_out("h1", block, regroup_by_tensor("h1", block, h1_tensor_cols(block)))
             if h1_scalar_cols(block) > 0:
                 grouped_tile("h1", block)
-                dst, src = regrouping_views("h1", block, slice(0, h1_scalar_cols(block)))
+                first = h1_tensor_cols(block)
+                dst, src = regrouping_views("h1", block, slice(first, first + h1_scalar_cols(block)))
                 nc.scalar.copy(out=dst, in_=src)
 
         def regroup_on_vector(block):
             names = ACTIVATIONS if block < PREP_LEAD else ("h0", "h1")
             for name in names:
                 grouped_tile(name, block)
-                first = h1_scalar_cols(block) if name == "h1" else 0
+                first = h1_tensor_cols(block) + h1_scalar_cols(block) if name == "h1" else 0
                 dst, src = regrouping_views(name, block, slice(first, BLOCK))
                 nc.vector.tensor_copy(out=dst, in_=src)
+            if block < PREP_LEAD:
+                load_input("x", block + LOAD_BUFS)
+            if block < FIRST_TENSOR:
+                load_h_ahead(block)
+
+        def load_h_ahead(block):
             if block + LOAD_BUFS < N_BLOCKS:
-                for name in names:
+                for name in ("h0", "h1"):
                     load_input(name, block + LOAD_BUFS)
 
         def quantise(block):
@@ -309,11 +336,17 @@ def tile_mdlstmcellweights_pb_t_kernel(
                 tanh_cell(following, 0)
             if ahead < N_BLOCKS:
                 regroup_x(ahead)
+            if SHARE_EARLY and FIRST_TENSOR <= ahead < N_BLOCKS:
+                scalar_share_of_h1(ahead)
             products(block, 0)
             if ahead < N_BLOCKS:
                 regroup_on_vector(ahead)
             total(block, 0)
             gate_half(block, 1)
+            if FIRST_TENSOR <= ahead < N_BLOCKS:
+                if not SHARE_EARLY:
+                    scalar_share_of_h1(ahead)
+                load_h_ahead(ahead)
             if following < LAST:
                 tanh_cell(following, 1)
             products(block, 1)

@@ -26,9 +26,8 @@ RUN = 4
 X_BANK = 256
 GATE_BANKS = 5
 H1_SCALAR_COLS = 0
-SHARE_EARLY = 0
 H1_TENSOR_COLS = 256
-FIRST_TENSOR = 3
+FIRST_TENSOR = 2
 LOAD_BUFS = 2
 PREP_LEAD = 2
 ACTIVATIONS = ("x", "h0", "h1")
@@ -147,17 +146,11 @@ def tile_mdlstmcellweights_pb_t_kernel(
                     out=flat[:, j * X_BANK * PACK : (j * X_BANK + width) * PACK], in_=bank[:, 0 : width * PACK]
                 )
 
-        def regroup_x(block):
-            if block < FIRST_TENSOR:
-                grouped_tile("x", block)
-                dst, src = regrouping_views("x", block, slice(0, BLOCK))
-                nc.scalar.copy(out=dst, in_=src)
-                load_input("x", block + LOAD_BUFS)
-                return
+        def x_by_tensor(block):
             banks = regroup_by_tensor("x", block, BLOCK)
             if block + LOAD_BUFS < N_BLOCKS:
                 load_input("x", block + LOAD_BUFS)
-            copy_out("x", block, banks)
+            return banks
 
         def scalar_share_of_h1(block):
             copy_out("h1", block, regroup_by_tensor("h1", block, h1_tensor_cols(block)))
@@ -334,20 +327,22 @@ def tile_mdlstmcellweights_pb_t_kernel(
             gate_half(block, 0)
             if following < LAST:
                 tanh_cell(following, 0)
-            if ahead < N_BLOCKS:
-                regroup_x(ahead)
-            if SHARE_EARLY and FIRST_TENSOR <= ahead < N_BLOCKS:
-                scalar_share_of_h1(ahead)
+            late_x = block == 0
+            if ahead < N_BLOCKS and not late_x:
+                copy_out("x", ahead, x_by_tensor(ahead))
             products(block, 0)
             if ahead < N_BLOCKS:
                 regroup_on_vector(ahead)
             total(block, 0)
             gate_half(block, 1)
-            if FIRST_TENSOR <= ahead < N_BLOCKS:
-                if not SHARE_EARLY:
-                    scalar_share_of_h1(ahead)
+            if late_x:
+                x_banks = x_by_tensor(ahead)
+                tanh_cell(following, 1)
+                copy_out("x", ahead, x_banks)
+            if ahead < N_BLOCKS:
+                scalar_share_of_h1(ahead)
                 load_h_ahead(ahead)
-            if following < LAST:
+            if following < LAST and not late_x:
                 tanh_cell(following, 1)
             products(block, 1)
             if ahead < N_BLOCKS:

@@ -25,7 +25,8 @@ HALF_TILES = M_TILES // 2
 RUN = 4
 X_BANK = 256
 GATE_BANKS = 5
-H1_SCALAR_COLS = 0
+H1_SCALAR_COLS = 64
+FIRST_SCALAR_SHARE = 4
 H1_TENSOR_COLS = 256
 FIRST_TENSOR = 2
 LOAD_BUFS = 2
@@ -119,7 +120,7 @@ def tile_mdlstmcellweights_pb_t_kernel(
             return 0 if block < FIRST_TENSOR else H1_TENSOR_COLS
 
         def h1_scalar_cols(block):
-            return 0 if block < FIRST_TENSOR else H1_SCALAR_COLS
+            return 0 if block < FIRST_SCALAR_SHARE else H1_SCALAR_COLS
 
         def regroup_by_tensor(name, block, n_cols):
             banks = {}
@@ -160,34 +161,35 @@ def tile_mdlstmcellweights_pb_t_kernel(
                 dst, src = regrouping_views("h1", block, slice(first, first + h1_scalar_cols(block)))
                 nc.scalar.copy(out=dst, in_=src)
 
+        def regroup_one(name, block):
+            grouped_tile(name, block)
+            first = h1_tensor_cols(block) + h1_scalar_cols(block) if name == "h1" else 0
+            dst, src = regrouping_views(name, block, slice(first, BLOCK))
+            nc.vector.tensor_copy(out=dst, in_=src)
+
         def regroup_on_vector(block):
-            names = ACTIVATIONS if block < PREP_LEAD else ("h0", "h1")
-            for name in names:
-                grouped_tile(name, block)
-                first = h1_tensor_cols(block) + h1_scalar_cols(block) if name == "h1" else 0
-                dst, src = regrouping_views(name, block, slice(first, BLOCK))
-                nc.vector.tensor_copy(out=dst, in_=src)
-            if block < PREP_LEAD:
-                load_input("x", block + LOAD_BUFS)
-            if block < FIRST_TENSOR:
-                load_h_ahead(block)
+            for name in ("h0", "h1"):
+                regroup_one(name, block)
 
         def load_h_ahead(block):
             if block + LOAD_BUFS < N_BLOCKS:
                 for name in ("h0", "h1"):
                     load_input(name, block + LOAD_BUFS)
 
+        def quantise_one(name, block):
+            words = packed.tile([P, BLOCK], U32, name="codes_" + name, tag="codes_" + name, align_bytes=64)
+            plane = packed.tile([P, BLOCK], U8, name="scales_" + name, tag="scales_" + name, align_bytes=64)
+            nc.vector.quantize_mx(
+                out=words[:].bitcast(FP8X4),
+                scales=plane[:],
+                in_=grouped[(name, block)][:].rearrange("p n t -> p (n t)"),
+            )
+            codes[(name, block)] = words
+            scales[(name, block)] = plane
+
         def quantise(block):
             for name in ACTIVATIONS:
-                words = packed.tile([P, BLOCK], U32, name="codes_" + name, tag="codes_" + name, align_bytes=64)
-                plane = packed.tile([P, BLOCK], U8, name="scales_" + name, tag="scales_" + name, align_bytes=64)
-                nc.vector.quantize_mx(
-                    out=words[:].bitcast(FP8X4),
-                    scales=plane[:],
-                    in_=grouped[(name, block)][:].rearrange("p n t -> p (n t)"),
-                )
-                codes[(name, block)] = words
-                scales[(name, block)] = plane
+                quantise_one(name, block)
 
         def tanh_cell(block, d):
             result = tanhs.tile([P, M_TILES, BLOCK], F32, name="tanh_%d" % d, tag="tanh_%d" % d)
@@ -299,14 +301,22 @@ def tile_mdlstmcellweights_pb_t_kernel(
                 nc.sync.dma_start(out=mix_row[0:1, :], in_=weighted_sum.rearrange("(o d) -> o d", o=1))
             for key in ("io", "ho"):
                 load_weight_piece(key, piece)
-        for name in ("x", "h0", "h1", "c0"):
+        for name in ("x", "h0", "c0", "h1", "c1"):
             load_input(name, 1)
 
-        regroup_on_vector(0)
-        load_input("c1", 1)
-        quantise(0)
-        for d in DIRECTIONS:
-            tanh_cell(0, d)
+        def gate_direction(block, d):
+            for m in range(M_TILES):
+                gate_tile(block, d, m)
+
+        def load_activations(block):
+            for name in ACTIVATIONS:
+                load_input(name, block)
+
+        regroup_one("x", 0)
+        regroup_one("h0", 0)
+        quantise_one("x", 0)
+        quantise_one("h0", 0)
+        regroup_one("h1", 0)
 
         spread = psum.tile([P, M_TILES + 2], F32, name="spread", tag="acc")
         nc.tensor.matmul(out=spread[:, 0:M_TILES], lhsT=bias_rows[:], rhs=pick[:], start=True, stop=True)
@@ -316,33 +326,71 @@ def tile_mdlstmcellweights_pb_t_kernel(
         bias = small[:, 0:M_TILES]
         mix = small[:, M_TILES : M_TILES + 2]
 
-        for block in range(1, PREP_LEAD):
-            regroup_on_vector(block)
-            quantise(block)
+        quantise_one("h1", 0)
+        load_activations(2)
+        tanh_cell(0, 0)
+        tanh_cell(0, 1)
+        gate_direction(0, 0)
+        gate_direction(0, 1)
+
+        regroup_one("x", 1)
+        regroup_one("h0", 1)
+        quantise_one("x", 1)
+        quantise_one("h0", 1)
+        product(0, 0, 0)
+        product(0, 0, 1)
+        regroup_one("h1", 1)
+        product(0, 1, 0)
+        quantise_one("h1", 1)
+        load_activations(3)
+        tanh_cell(1, 0)
+        gate_direction(1, 0)
+
+        total(0, 0)
+        product(0, 1, 1)
+        copy_out("x", 2, x_by_tensor(2))
+        tanh_cell(1, 1)
+        gate_direction(1, 1)
+
+        regroup_one("h0", 2)
+        total(0, 1)
+        regroup_one("h1", 2)
+        scalar_share_of_h1(2)
+        load_h_ahead(2)
+        product(1, 0, 0)
+        quantise(2)
+        tanh_cell(2, 0)
+        product(1, 0, 1)
+        copy_out("x", 3, x_by_tensor(3))
+        tanh_cell(2, 1)
+        product(1, 1, 0)
+        regroup_one("h0", 3)
+        total(1, 0)
+        product(1, 1, 1)
+        regroup_one("h1", 3)
+        total(1, 1)
+        scalar_share_of_h1(3)
+        load_h_ahead(3)
+        quantise(3)
 
         LAST = N_BLOCKS - 1
-        for block in range(LAST):
+        for block in range(2, LAST):
             following = block + 1
             ahead = block + PREP_LEAD
             gate_half(block, 0)
             if following < LAST:
                 tanh_cell(following, 0)
-            late_x = block == 0
-            if ahead < N_BLOCKS and not late_x:
+            if ahead < N_BLOCKS:
                 copy_out("x", ahead, x_by_tensor(ahead))
             products(block, 0)
             if ahead < N_BLOCKS:
                 regroup_on_vector(ahead)
             total(block, 0)
             gate_half(block, 1)
-            if late_x:
-                x_banks = x_by_tensor(ahead)
-                tanh_cell(following, 1)
-                copy_out("x", ahead, x_banks)
             if ahead < N_BLOCKS:
                 scalar_share_of_h1(ahead)
                 load_h_ahead(ahead)
-            if following < LAST and not late_x:
+            if following < LAST:
                 tanh_cell(following, 1)
             products(block, 1)
             if ahead < N_BLOCKS:

@@ -29,6 +29,7 @@ H1_SCALAR_COLS = 64
 FIRST_SCALAR_SHARE = 4
 H1_TENSOR_COLS = 256
 FIRST_TENSOR = 2
+END_PIECES = 2
 LOAD_BUFS = 2
 PREP_LEAD = 2
 ACTIVATIONS = ("x", "h0", "h1")
@@ -289,6 +290,8 @@ def tile_mdlstmcellweights_pb_t_kernel(
         nc.vector.memset(ones[:], 1.0)
         ident = consts.tile([P, P], BF16, name="ident")
         make_identity(nc, ident[:])
+        ident_f32 = consts.tile([P, P], F32, name="ident_f32")
+        make_identity(nc, ident_f32[:])
         pick = consts.tile([P, M_TILES], BF16, name="pick")
         nc.vector.memset(pick[:], 0.0)
         for m in range(M_TILES):
@@ -404,7 +407,25 @@ def tile_mdlstmcellweights_pb_t_kernel(
             for d in DIRECTIONS:
                 gate_tile(LAST, d, m)
             product(LAST, 0, half, i, i + 1)
-            if m > 0:
+            if m > 1:
                 total(LAST, (m - 1) // HALF_TILES, (m - 1) % HALF_TILES, (m - 1) % HALF_TILES + 1)
             product(LAST, 1, half, i, i + 1)
-        total(LAST, 1, HALF_TILES - 1, HALF_TILES)
+        first_sum = psum.tile([P, BLOCK], F32, name="acc", tag="acc")
+        for d in DIRECTIONS:
+            nc.tensor.matmul(
+                out=first_sum[:], lhsT=ident_f32[:], rhs=gate[(d, LAST, 0)][:, 0, :], start=(d == 0), stop=(d == 1)
+            )
+        nc.scalar.copy(out=gate[(0, LAST, 0)][:, 0, :], in_=first_sum[:])
+        nc.scalar.dma_start(out=out_dram[:, 0, block_cols(LAST)], in_=gate[(0, LAST, 0)][:, 0, :])
+        for piece in range(END_PIECES):
+            cols = slice(piece * BLOCK // END_PIECES, (piece + 1) * BLOCK // END_PIECES)
+            nc.vector.tensor_tensor(
+                out=gate[(0, LAST, 1)][:, HALF_TILES - 1, cols],
+                in0=gate[(0, LAST, 1)][:, HALF_TILES - 1, cols],
+                in1=gate[(1, LAST, 1)][:, HALF_TILES - 1, cols],
+                op=ALU.add,
+            )
+            nc.sync.dma_start(
+                out=out_dram[:, M_TILES - 1, LAST * BLOCK + cols.start : LAST * BLOCK + cols.stop],
+                in_=gate[(0, LAST, 1)][:, HALF_TILES - 1, cols],
+            )

@@ -25,7 +25,7 @@ HALF_TILES = M_TILES // 2
 RUN = 4
 X_BANK = 256
 GATE_BANKS = 5
-H1_SCALAR_COLS = 64
+H1_SCALAR_COLS = 32
 FIRST_SCALAR_SHARE = 4
 H1_TENSOR_COLS = 256
 FIRST_TENSOR = 2

from contextlib import ExitStack

import concourse.mybir as mybir
from concourse.masks import make_identity

F32 = mybir.dt.float32
BF16 = mybir.dt.bfloat16
I32 = mybir.dt.int32
U32 = mybir.dt.uint32
U8 = mybir.dt.uint8
FP8X4 = mybir.dt.float8_e4m3fn_x4
FP4X4 = mybir.dt.float4_e2m1fn_x4
ACT = mybir.ActivationFunctionType
ALU = mybir.AluOpType

P = 128
PACK = 4
CHANNELS = 512
POSITIONS = 4096
M_TILES = CHANNELS // P
assert M_TILES == PACK
BLOCK = 512
N_BLOCKS = POSITIONS // BLOCK
HALF_TILES = M_TILES // 2
RUN = 4
X_BANK = 256
GATE_BANKS = 5
H1_SCALAR_COLS = 32
FIRST_SCALAR_SHARE = 4
H1_TENSOR_COLS = 256
FIRST_TENSOR = 2
END_PIECES = 2
LOAD_BUFS = 2
PREP_LEAD = 2
ACTIVATIONS = ("x", "h0", "h1")
DIRECTIONS = (0, 1)

FLOPS = 3 * 2 * CHANNELS * CHANNELS * POSITIONS


def tile_mdlstmcellweights_pb_t_kernel(
    tc,
    x,
    h_prev_dim0,
    h_prev_dim1,
    ct0,
    ct1,
    w_io_words,
    w_io_scales,
    w_ho_words,
    w_ho_scales,
    b_o,
    weighted_sum,
    out,
):
    nc = tc.nc

    in_dram = {
        "x": x.rearrange("(p t) n -> p t n", t=PACK),
        "h0": h_prev_dim0.rearrange("(p t) n -> p t n", t=PACK),
        "h1": h_prev_dim1.rearrange("(p t) n -> p t n", t=PACK),
        "c0": ct0.rearrange("(m p) n -> p m n", p=P),
        "c1": ct1.rearrange("(m p) n -> p m n", p=P),
    }
    out_dram = out.rearrange("(m p) n -> p m n", p=P)
    weight_dram = {
        "io": (w_io_words.rearrange("g p b -> (g p) b"), w_io_scales.rearrange("g q n -> (g q) n")),
        "ho": (w_ho_words.rearrange("g p b -> (g p) b"), w_ho_scales.rearrange("g q n -> (g q) n")),
    }

    with ExitStack() as stack:
        consts = stack.enter_context(tc.tile_pool(name="consts", bufs=1))
        loads = stack.enter_context(tc.tile_pool(name="loads", bufs=LOAD_BUFS))
        groups = stack.enter_context(tc.tile_pool(name="groups", bufs=2))
        packed = stack.enter_context(tc.tile_pool(name="packed", bufs=PREP_LEAD + 2))
        tanhs = stack.enter_context(tc.tile_pool(name="tanhs", bufs=3))
        gates = stack.enter_context(tc.tile_pool(name="gates", bufs=4))
        psum = stack.enter_context(tc.psum_pool(name="psum", bufs=GATE_BANKS))
        xpsum = stack.enter_context(tc.psum_pool(name="xpsum", bufs=8 - GATE_BANKS))
        stack.enter_context(tc.manual_schedule())

        raw = {}
        grouped = {}
        codes = {}
        scales = {}
        tanh_c = {}
        gate = {}

        def block_cols(block):
            return slice(block * BLOCK, (block + 1) * BLOCK)

        def load_input(name, block):
            landed = loads.tile([P, PACK, BLOCK], BF16, name="raw_" + name, tag="raw_" + name)
            nc.sync.dma_start(out=landed[:], in_=in_dram[name][:, :, block_cols(block)])
            raw[(name, block)] = landed

        def load_weight_piece(key, piece):
            words, rows = weight_dram[key]
            if piece == 0:
                nc.sync.dma_start(out=w_words[key][:].bitcast(I32), in_=words.bitcast(I32))
            else:
                quadrant = piece - 1
                nc.sync.dma_start(
                    out=w_planes[key][32 * quadrant : 32 * quadrant + 4, :].bitcast(I32),
                    in_=rows[4 * quadrant : 4 * quadrant + 4, :].bitcast(I32),
                )

        def regrouping_views(name, block, cols):
            src = raw[(name, block)][:, :, cols].rearrange("p t (c i) -> p c t i", i=RUN)
            dst = grouped[(name, block)][:, cols, :].rearrange("p (c i) t -> p c t i", i=RUN)
            return dst, src

        def grouped_tile(name, block):
            if (name, block) not in grouped:
                grouped[(name, block)] = groups.tile(
                    [P, BLOCK, PACK], BF16, name="grouped_" + name, tag="grouped_" + name, align_bytes=64
                )
            return grouped[(name, block)]

        def h1_tensor_cols(block):
            return 0 if block < FIRST_TENSOR else H1_TENSOR_COLS

        def h1_scalar_cols(block):
            return 0 if block < FIRST_SCALAR_SHARE else H1_SCALAR_COLS

        def regroup_by_tensor(name, block, n_cols):
            banks = {}
            for j in range((n_cols + X_BANK - 1) // X_BANK):
                width = min(X_BANK, n_cols - j * X_BANK)
                bank = xpsum.tile([P, X_BANK * PACK], BF16, name="xbank", tag="xbank")
                for i in range(width // P):
                    cols = slice(j * X_BANK + i * P, j * X_BANK + (i + 1) * P)
                    nc.tensor.matmul(
                        out=bank[:, i * P * PACK : (i + 1) * P * PACK],
                        lhsT=ident[:],
                        rhs=raw[(name, block)][:, :, cols].rearrange("p t n -> p n t"),
                        start=True,
                        stop=True,
                    )
                banks[j] = (bank, width)
            return banks

        def copy_out(name, block, banks):
            flat = grouped_tile(name, block)[:].rearrange("p n t -> p (n t)")
            for j in range(len(banks)):
                bank, width = banks[j]
                nc.scalar.copy(
                    out=flat[:, j * X_BANK * PACK : (j * X_BANK + width) * PACK], in_=bank[:, 0 : width * PACK]
                )

        def x_by_tensor(block):
            banks = regroup_by_tensor("x", block, BLOCK)
            if block + LOAD_BUFS < N_BLOCKS:
                load_input("x", block + LOAD_BUFS)
            return banks

        def scalar_share_of_h1(block):
            copy_out("h1", block, regroup_by_tensor("h1", block, h1_tensor_cols(block)))
            if h1_scalar_cols(block) > 0:
                grouped_tile("h1", block)
                first = h1_tensor_cols(block)
                dst, src = regrouping_views("h1", block, slice(first, first + h1_scalar_cols(block)))
                nc.scalar.copy(out=dst, in_=src)

        def regroup_one(name, block):
            grouped_tile(name, block)
            first = h1_tensor_cols(block) + h1_scalar_cols(block) if name == "h1" else 0
            dst, src = regrouping_views(name, block, slice(first, BLOCK))
            nc.vector.tensor_copy(out=dst, in_=src)

        def regroup_on_vector(block):
            for name in ("h0", "h1"):
                regroup_one(name, block)

        def load_h_ahead(block):
            if block + LOAD_BUFS < N_BLOCKS:
                for name in ("h0", "h1"):
                    load_input(name, block + LOAD_BUFS)

        def quantise_one(name, block):
            words = packed.tile([P, BLOCK], U32, name="codes_" + name, tag="codes_" + name, align_bytes=64)
            plane = packed.tile([P, BLOCK], U8, name="scales_" + name, tag="scales_" + name, align_bytes=64)
            nc.vector.quantize_mx(
                out=words[:].bitcast(FP8X4),
                scales=plane[:],
                in_=grouped[(name, block)][:].rearrange("p n t -> p (n t)"),
            )
            codes[(name, block)] = words
            scales[(name, block)] = plane

        def quantise(block):
            for name in ACTIVATIONS:
                quantise_one(name, block)

        def tanh_cell(block, d):
            result = tanhs.tile([P, M_TILES, BLOCK], F32, name="tanh_%d" % d, tag="tanh_%d" % d)
            nc.scalar.activation(out=result[:], in_=raw[("c%d" % d, block)][:], func=ACT.Tanh)
            tanh_c[(d, block)] = result
            if block + LOAD_BUFS < N_BLOCKS:
                load_input("c%d" % d, block + LOAD_BUFS)

        def gate_tile(block, d, m):
            half, i = divmod(m, HALF_TILES)
            if (d, block, half) not in gate:
                gate[(d, block, half)] = gates.tile(
                    [P, HALF_TILES, BLOCK], F32, name="gate_%d" % d, tag="gate_%d" % d
                )
            h = "h%d" % d
            word_cols = slice(m * P * 2, (m + 1) * P * 2)
            plane_cols = slice(m * P, (m + 1) * P)
            acc = psum.tile([P, BLOCK], F32, name="acc", tag="acc")
            nc.tensor.matmul_mx(
                out=acc[:],
                lhsT=w_words["io"][:, word_cols].bitcast(FP4X4),
                lhsT_scale=w_planes["io"][:, plane_cols],
                rhs=codes[("x", block)][:].bitcast(FP8X4),
                rhs_scale=scales[("x", block)][:],
                start=True,
                stop=False,
            )
            nc.tensor.matmul_mx(
                out=acc[:],
                lhsT=w_words["ho"][:, word_cols].bitcast(FP4X4),
                lhsT_scale=w_planes["ho"][:, plane_cols],
                rhs=codes[(h, block)][:].bitcast(FP8X4),
                rhs_scale=scales[(h, block)][:],
                start=False,
                stop=True,
            )
            nc.scalar.activation(
                out=gate[(d, block, half)][:, i, :],
                in_=acc[:],
                func=ACT.Sigmoid,
                bias=bias[:, m : m + 1],
                scale=1.0,
            )

        def gate_half(block, half):
            for d in DIRECTIONS:
                for i in range(HALF_TILES):
                    gate_tile(block, d, half * HALF_TILES + i)

        def tanh_tile(block, d, m):
            if (d, block) not in tanh_c:
                tanh_c[(d, block)] = tanhs.tile([P, M_TILES, BLOCK], F32, name="tanh_%d" % d, tag="tanh_%d" % d)
            nc.scalar.activation(
                out=tanh_c[(d, block)][:, m, :], in_=raw[("c%d" % d, block)][:, m, :], func=ACT.Tanh
            )

        def product(block, d, half, first=0, last=HALF_TILES):
            tiles = slice(half * HALF_TILES + first, half * HALF_TILES + last)
            nc.vector.scalar_tensor_tensor(
                out=gate[(d, block, half)][:, first:last, :],
                in0=gate[(d, block, half)][:, first:last, :],
                scalar=mix[:, d : d + 1],
                in1=tanh_c[(d, block)][:, tiles, :],
                op0=ALU.mult,
                op1=ALU.mult,
            )

        def products(block, half):
            for d in DIRECTIONS:
                product(block, d, half)

        def total(block, half, first=0, last=HALF_TILES):
            tiles = slice(half * HALF_TILES + first, half * HALF_TILES + last)
            nc.vector.tensor_tensor(
                out=gate[(0, block, half)][:, first:last, :],
                in0=gate[(0, block, half)][:, first:last, :],
                in1=gate[(1, block, half)][:, first:last, :],
                op=ALU.add,
            )
            nc.sync.dma_start(out=out_dram[:, tiles, block_cols(block)], in_=gate[(0, block, half)][:, first:last, :])

        warm = consts.tile([P, 1], F32, name="warm")
        nc.vector.memset(warm[:], 0.0)
        nc.scalar.activation(out=warm[:], in_=warm[:], func=ACT.Sigmoid)

        w_words = {}
        w_planes = {}
        for key in ("io", "ho"):
            w_words[key] = consts.tile([P, 2 * CHANNELS], U8, name="words_" + key, align_bytes=64)
            w_planes[key] = consts.tile([P, CHANNELS], U8, name="planes_" + key, align_bytes=64)
            nc.vector.memset(w_planes[key][:].bitcast(I32), 0)
        bias_rows = consts.tile([P, P], BF16, name="bias_rows")
        nc.vector.memset(bias_rows[:], 0.0)
        mix_row = consts.tile([P, 2], BF16, name="mix_row")
        nc.vector.memset(mix_row[:], 0.0)
        ones = consts.tile([P, P], BF16, name="ones")
        nc.vector.memset(ones[:], 1.0)
        ident = consts.tile([P, P], BF16, name="ident")
        make_identity(nc, ident[:])
        ident_f32 = consts.tile([P, P], F32, name="ident_f32")
        make_identity(nc, ident_f32[:])
        pick = consts.tile([P, M_TILES], BF16, name="pick")
        nc.vector.memset(pick[:], 0.0)
        for m in range(M_TILES):
            nc.vector.memset(pick[32 * m : 32 * (m + 1), m : m + 1], 1.0)

        for piece, name in enumerate(("x", "h0", "c0", "h1", "c1")):
            load_input(name, 0)
            if piece == 0:
                nc.sync.dma_start(out=bias_rows[0:P:32, :], in_=b_o.rearrange("(m p) o -> m (p o)", p=P))
                nc.sync.dma_start(out=mix_row[0:1, :], in_=weighted_sum.rearrange("(o d) -> o d", o=1))
            for key in ("io", "ho"):
                load_weight_piece(key, piece)
        for name in ("x", "h0", "c0", "h1", "c1"):
            load_input(name, 1)

        def gate_direction(block, d):
            for m in range(M_TILES):
                gate_tile(block, d, m)

        def load_activations(block):
            for name in ACTIVATIONS:
                load_input(name, block)

        regroup_one("x", 0)
        regroup_one("h0", 0)
        quantise_one("x", 0)
        quantise_one("h0", 0)
        regroup_one("h1", 0)

        spread = psum.tile([P, M_TILES + 2], F32, name="spread", tag="acc")
        nc.tensor.matmul(out=spread[:, 0:M_TILES], lhsT=bias_rows[:], rhs=pick[:], start=True, stop=True)
        nc.tensor.matmul(out=spread[:, M_TILES : M_TILES + 2], lhsT=ones[:], rhs=mix_row[:], start=True, stop=True)
        small = consts.tile([P, M_TILES + 2], F32, name="small")
        nc.vector.tensor_copy(out=small[:], in_=spread[:])
        bias = small[:, 0:M_TILES]
        mix = small[:, M_TILES : M_TILES + 2]

        quantise_one("h1", 0)
        load_activations(2)
        tanh_cell(0, 0)
        tanh_cell(0, 1)
        gate_direction(0, 0)
        gate_direction(0, 1)

        regroup_one("x", 1)
        regroup_one("h0", 1)
        quantise_one("x", 1)
        quantise_one("h0", 1)
        product(0, 0, 0)
        product(0, 0, 1)
        regroup_one("h1", 1)
        product(0, 1, 0)
        quantise_one("h1", 1)
        load_activations(3)
        tanh_cell(1, 0)
        gate_direction(1, 0)

        total(0, 0)
        product(0, 1, 1)
        copy_out("x", 2, x_by_tensor(2))
        tanh_cell(1, 1)
        gate_direction(1, 1)

        regroup_one("h0", 2)
        total(0, 1)
        regroup_one("h1", 2)
        scalar_share_of_h1(2)
        load_h_ahead(2)
        product(1, 0, 0)
        quantise(2)
        tanh_cell(2, 0)
        product(1, 0, 1)
        copy_out("x", 3, x_by_tensor(3))
        tanh_cell(2, 1)
        product(1, 1, 0)
        regroup_one("h0", 3)
        total(1, 0)
        product(1, 1, 1)
        regroup_one("h1", 3)
        total(1, 1)
        scalar_share_of_h1(3)
        load_h_ahead(3)
        quantise(3)

        LAST = N_BLOCKS - 1
        for block in range(2, LAST):
            following = block + 1
            ahead = block + PREP_LEAD
            gate_half(block, 0)
            if following < LAST:
                tanh_cell(following, 0)
            if ahead < N_BLOCKS:
                copy_out("x", ahead, x_by_tensor(ahead))
            products(block, 0)
            if ahead < N_BLOCKS:
                regroup_on_vector(ahead)
            total(block, 0)
            gate_half(block, 1)
            if ahead < N_BLOCKS:
                scalar_share_of_h1(ahead)
                load_h_ahead(ahead)
            if following < LAST:
                tanh_cell(following, 1)
            products(block, 1)
            if ahead < N_BLOCKS:
                quantise(ahead)
            total(block, 1)

        for m in range(M_TILES):
            half, i = divmod(m, HALF_TILES)
            for d in DIRECTIONS:
                tanh_tile(LAST, d, m)
            for d in DIRECTIONS:
                gate_tile(LAST, d, m)
            product(LAST, 0, half, i, i + 1)
            if m > 1:
                total(LAST, (m - 1) // HALF_TILES, (m - 1) % HALF_TILES, (m - 1) % HALF_TILES + 1)
            product(LAST, 1, half, i, i + 1)
        first_sum = psum.tile([P, BLOCK], F32, name="acc", tag="acc")
        for d in DIRECTIONS:
            nc.tensor.matmul(
                out=first_sum[:], lhsT=ident_f32[:], rhs=gate[(d, LAST, 0)][:, 0, :], start=(d == 0), stop=(d == 1)
            )
        nc.scalar.copy(out=gate[(0, LAST, 0)][:, 0, :], in_=first_sum[:])
        nc.scalar.dma_start(out=out_dram[:, 0, block_cols(LAST)], in_=gate[(0, LAST, 0)][:, 0, :])
        for piece in range(END_PIECES):
            cols = slice(piece * BLOCK // END_PIECES, (piece + 1) * BLOCK // END_PIECES)
            nc.vector.tensor_tensor(
                out=gate[(0, LAST, 1)][:, HALF_TILES - 1, cols],
                in0=gate[(0, LAST, 1)][:, HALF_TILES - 1, cols],
                in1=gate[(1, LAST, 1)][:, HALF_TILES - 1, cols],
                op=ALU.add,
            )
            nc.sync.dma_start(
                out=out_dram[:, M_TILES - 1, LAST * BLOCK + cols.start : LAST * BLOCK + cols.stop],
                in_=gate[(0, LAST, 1)][:, HALF_TILES - 1, cols],
            )
